import numpy as np
import ml_dtypes


def mxq(x, axis, fmt="e4m3"):
    dtype, down = {"e4m3": (ml_dtypes.float8_e4m3fn, 7), "e5m2": (ml_dtypes.float8_e5m2, 14)}[fmt]
    v = np.moveaxis(np.asarray(x, np.float32).astype(ml_dtypes.bfloat16).astype(np.float64), axis, -1)
    blocks = v.reshape(v.shape[:-1] + (-1, 32))
    amax = np.abs(blocks).max(-1, keepdims=True)
    byte = np.maximum(np.where(amax > 0, np.frexp(amax)[1] - 1 + 127, 0) - down, 1)
    scale = np.exp2(byte - 127.0)
    codes = (blocks / scale).astype(np.float32).astype(dtype).astype(np.float64)
    return np.moveaxis((codes * scale).reshape(v.shape), -1, axis)


WIDE = False


def mx_kscale(k):
    if not WIDE:
        return np.ones(k)
    levels = np.array([10, -10, 5, -5, 0])
    a = np.random.permutation(np.resize(levels, k // 512 * 4)).reshape(k // 512, 4)
    idx = np.arange(k)
    return np.exp2(a[idx // 512, idx % 128 // 32])


BF16 = ml_dtypes.bfloat16


def bf(x):
    return np.asarray(x, np.float32).astype(BF16)


def f64(x):
    return np.asarray(x).astype(np.float64)


N, C, I = 512, 128, 8
EPS = 1e-5


def sigmoid(v):
    return 1.0 / (1.0 + np.exp(-v))


def layernorm(x, g, b):
    mu = x.mean(-1, keepdims=True)
    var = np.square(x - mu).mean(-1, keepdims=True)
    return (x - mu) / np.sqrt(var + EPS) * g + b


def setup_inputs():
    s = mx_kscale(N)[None, :, None]
    return {"left_proj": bf(np.random.standard_normal((N, N, I)) * s),
            "left_gate": bf(np.random.standard_normal((N, N, I))),
            "right_proj": bf(np.random.standard_normal((N, N, I)) / s),
            "right_gate": bf(np.random.standard_normal((N, N, I))),
            "mask": bf(np.random.uniform(size=(N, N)) > 0.5),
            "ln_c_g": bf(1.0 + 0.1 * np.random.standard_normal(I)),
            "ln_c_b": bf(0.1 * np.random.standard_normal(I))}


def reference(left_proj, left_gate, right_proj, right_gate, mask, ln_c_g, ln_c_b):
    m = f64(mask)[..., None]
    left = m * f64(left_proj) * sigmoid(f64(left_gate))
    right = m * f64(right_proj) * sigmoid(f64(right_gate))
    lt = left.transpose(2, 0, 1)
    rt = right.transpose(2, 1, 0)
    x = (mxq(lt, 2, "e4m3") @ mxq(rt, 1, "e4m3")).transpose(1, 2, 0)
    return layernorm(x, f64(ln_c_g), f64(ln_c_b))

@@ -1,0 +1,235 @@
+from contextlib import ExitStack
+
+import concourse.mybir as mybir
+from concourse.masks import make_identity
+
+BF16 = mybir.dt.bfloat16
+F32 = mybir.dt.float32
+U32 = mybir.dt.uint32
+U8 = mybir.dt.uint8
+FP8X4 = mybir.dt.float8_e4m3fn_x4
+ACT = mybir.ActivationFunctionType
+ALU = mybir.AluOpType
+
+P = 128
+PACK = 4
+RES = 512
+CH = 8
+PAIRS = CH // 2
+TILES = RES // P
+HALF = RES // 2
+QUAD = 4
+EPS = 1e-5
+
+FLOPS = 2 * RES * RES * RES * CH
+
+
+def tile_net2_pa_kernel(
+    tc, left_proj, left_gate, right_proj, right_gate, mask, ln_c_g, ln_c_b, out
+):
+    nc = tc.nc
+    with ExitStack() as ctx:
+        ctx.enter_context(tc.manual_schedule())
+        keep = ctx.enter_context(tc.tile_pool(name="keep", bufs=1))
+        psum = ctx.enter_context(tc.psum_pool(name="psum", bufs=1))
+
+        ident_f32 = keep.tile([P, P], F32)
+        make_identity(nc, ident_f32)
+        ident_bf16 = keep.tile([P, P], BF16)
+        make_identity(nc, ident_bf16)
+
+        gain_bf16 = keep.tile([P, CH], BF16)
+        nc.scalar.dma_start(out=gain_bf16, in_=ln_c_g.partition_broadcast(P))
+        bias_bf16 = keep.tile([P, CH], BF16)
+        nc.scalar.dma_start(out=bias_bf16, in_=ln_c_b.partition_broadcast(P))
+        gain = keep.tile([P, CH], F32)
+        nc.vector.tensor_copy(out=gain, in_=gain_bf16)
+        bias = keep.tile([P, CH], F32)
+        nc.vector.tensor_copy(out=bias, in_=bias_bf16)
+        eps = keep.tile([P, 1], F32)
+        nc.vector.memset(eps, EPS)
+
+        left_codes = keep.tile([P, CH, RES], U32, align_bytes=64)
+        left_scales = keep.tile([P, CH, RES], U8, align_bytes=64)
+        right_codes = keep.tile([P, CH, RES], U32, align_bytes=64)
+        right_scales = keep.tile([P, CH, RES], U8, align_bytes=64)
+        mask_kt = keep.tile([P, TILES, P, PACK], BF16)
+
+        with tc.tile_pool(name="loads", bufs=3) as loads, tc.tile_pool(name="work", bufs=3) as work:
+            mask_rows = loads.tile([P, TILES, RES], BF16, bufs=1)
+            nc.sync.dma_start(out=mask_rows, in_=mask.rearrange("(n r) k -> r n k", r=P))
+            for n in range(TILES):
+                mask_t = psum.tile([P, PACK, P], BF16, tag="proj", bufs=2)
+                for t in range(PACK):
+                    nc.tensor.transpose(
+                        mask_t[:, t, :], mask_rows[:, n, t * P : (t + 1) * P], ident_bf16
+                    )
+                nc.scalar.copy(out=mask_kt[:, n], in_=mask_t.rearrange("p t r -> p r t"))
+
+            def transposed_pair(rows, w, tag, bufs):
+                words = rows.bitcast(F32).rearrange("r (k w) -> r k w", w=PAIRS)
+                bank = psum.tile([P, PACK, P], F32, tag=tag, bufs=bufs)
+                for t in range(PACK):
+                    nc.tensor.transpose(bank[:, t, :], words[:, t * P : (t + 1) * P, w], ident_f32)
+                return bank.bitcast(BF16).rearrange("p t (r e) -> p e r t", e=2)
+
+            sides = (
+                (right_proj, right_gate, right_codes, right_scales),
+                (left_proj, left_gate, left_codes, left_scales),
+            )
+            groups = [(s, n, w) for s in range(2) for n in range(TILES) for w in range(PAIRS)]
+            loaded = {}
+            gated = {}
+            masked = {}
+
+            def gate_group(g):
+                s, n, w = groups[g]
+                if w == 0:
+                    gate_rows = loads.tile([P, RES * CH], BF16, tag="gate_rows")
+                    proj_rows = loads.tile([P, RES * CH], BF16, tag="proj_rows")
+                    rows = slice(n * P, (n + 1) * P)
+                    nc.sync.dma_start(out=gate_rows, in_=sides[s][1][rows].rearrange("r k c -> r (k c)"))
+                    nc.sync.dma_start(out=proj_rows, in_=sides[s][0][rows].rearrange("r k c -> r (k c)"))
+                    loaded[(s, n)] = (proj_rows, gate_rows)
+                proj_rows, gate_rows = loaded[(s, n)]
+                gate_t = transposed_pair(gate_rows, w, "aux", 3)
+                proj_t = transposed_pair(proj_rows, w, "proj", 2)
+                sig = work.tile([P, 2, P, PACK], F32, tag="sig")
+                nc.scalar.activation(out=sig, in_=gate_t, func=ACT.Sigmoid)
+                product = work.tile([P, 2, P, PACK], BF16, tag="product")
+                nc.vector.tensor_tensor(out=product, in0=proj_t, in1=sig, op=ALU.mult)
+                gated[g] = product
+
+            def mask_group(g):
+                s, n, w = groups[g]
+                kept = work.tile([P, 2, P, PACK], BF16, tag="kept", align_bytes=64)
+                nc.vector.tensor_tensor(
+                    out=kept,
+                    in0=gated[g],
+                    in1=mask_kt[:, n].unsqueeze(1).to_broadcast([P, 2, P, PACK]),
+                    op=ALU.mult,
+                )
+                masked[g] = kept
+
+            def quantise_group(g):
+                s, n, w = groups[g]
+                rows = slice(n * P, (n + 1) * P)
+                for e in range(2):
+                    nc.vector.quantize_mx(
+                        out=sides[s][2][:, 2 * w + e, rows].bitcast(FP8X4),
+                        scales=sides[s][3][:, 2 * w + e, rows],
+                        in_=masked[g][:, e].rearrange("p r t -> p (r t)"),
+                    )
+
+            for g in range(len(groups) + 2):
+                if g < len(groups):
+                    gate_group(g)
+                if 1 <= g <= len(groups):
+                    mask_group(g - 1)
+                if g >= 2:
+                    quantise_group(g - 2)
+
+        with tc.tile_pool(name="norm", bufs=2) as norm:
+            means = {}
+            planes = {}
+            squares = {}
+            rstds = {}
+
+            def product_pass(acc, a, c, start, stop):
+                rows = slice(a * P, (a + 1) * P)
+                nc.tensor.matmul_mx(
+                    out=acc,
+                    lhsT=left_codes[:, c, rows].bitcast(FP8X4),
+                    lhsT_scale=left_scales[:, c, rows],
+                    rhs=right_codes[:, c, :].bitcast(FP8X4),
+                    rhs_scale=right_scales[:, c, :],
+                    start=start,
+                    stop=stop,
+                )
+
+            def mean_rows(a):
+                total = psum.tile([P, RES], F32, tag="sum", bufs=1)
+                for c in range(CH):
+                    product_pass(total, a, c, c == 0, c == CH - 1)
+                mean = norm.tile([P, RES], F32, tag="mean")
+                nc.scalar.activation(out=mean, in_=total, func=ACT.Copy, scale=1.0 / CH)
+                means[a] = mean
+
+            def centre_rows(a):
+                centred = norm.tile([P, CH, RES], F32, tag="centred", bufs=3)
+                squared = norm.tile([P, CH, RES], F32, tag="squared")
+                for c in range(CH):
+                    x = psum.tile([P, RES], F32, tag="x", bufs=2)
+                    product_pass(x, a, c, True, True)
+                    nc.vector.tensor_tensor(out=centred[:, c, :], in0=x, in1=means[a], op=ALU.subtract)
+                    if c % 2 == 1:
+                        nc.scalar.activation(
+                            out=squared[:, c - 1 : c + 1, :], in_=centred[:, c - 1 : c + 1, :], func=ACT.Square
+                        )
+                planes[a] = centred
+                squares[a] = squared
+
+            def rstd_rows(a):
+                var_t = psum.tile([P, TILES, P], F32, tag="aux", bufs=3)
+                for b in range(TILES):
+                    for c in range(CH):
+                        nc.tensor.matmul(
+                            out=var_t[:, b, :],
+                            lhsT=squares[a][:, c, b * P : (b + 1) * P],
+                            rhs=ident_f32,
+                            is_transpose=True,
+                            start=(c == 0),
+                            stop=(c == CH - 1),
+                        )
+                rstd_t = norm.tile([P, TILES, P], F32, tag="rstd_t")
+                nc.scalar.activation(
+                    out=rstd_t, in_=var_t, func=ACT.Abs_reciprocal_sqrt, scale=1.0 / CH, bias=eps
+                )
+                rstd = psum.tile([P, TILES, P], F32, tag="aux", bufs=3)
+                for b in range(TILES):
+                    nc.tensor.transpose(rstd[:, b, :], rstd_t[:, b, :], ident_f32)
+                rstds[a] = rstd.rearrange("p b j -> p (b j)")
+
+            def normalise_rows(a):
+                centred = planes[a]
+                halves = [slice(h * HALF, (h + 1) * HALF) for h in range(RES // HALF)]
+                for cols in halves:
+                    nc.vector.tensor_tensor(
+                        out=centred[:, :, cols],
+                        in0=centred[:, :, cols],
+                        in1=rstds[a][:, cols].unsqueeze(1).to_broadcast([P, CH, HALF]),
+                        op=ALU.mult,
+                    )
+                for cols in halves:
+                    for c in range(CH):
+                        nc.vector.tensor_scalar(
+                            out=centred[:, c, cols],
+                            in0=centred[:, c, cols],
+                            scalar1=gain[:, c : c + 1],
+                            scalar2=bias[:, c : c + 1],
+                            op0=ALU.mult,
+                            op1=ALU.add,
+                        )
+                    result = norm.tile([P, HALF, CH], F32, tag="result", bufs=3)
+                    for q in range(0, CH, QUAD):
+                        nc.scalar.copy(
+                            out=result[:, :, q : q + QUAD],
+                            in_=centred[:, q : q + QUAD, cols].rearrange("p c j -> p j c"),
+                        )
+                    nc.sync.dma_start(
+                        out=out[a * P : (a + 1) * P, cols, :].rearrange("i j c -> i (j c)"),
+                        in_=result.rearrange("p j c -> p (j c)"),
+                    )
+
+            mean_rows(0)
+            centre_rows(0)
+            mean_rows(1)
+            rstd_rows(0)
+            for a in range(TILES):
+                if a + 1 < TILES:
+                    centre_rows(a + 1)
+                if a + 2 < TILES:
+                    mean_rows(a + 2)
+                if a + 1 < TILES:
+                    rstd_rows(a + 1)
+                normalise_rows(a)

@@ -19,6 +19,8 @@ PAIRS = CH // 2
 TILES = RES // P
 HALF = RES // 2
 QUAD = 4
+LEAD = 2
+BANKS = 6
 EPS = 1e-5
 
 FLOPS = 2 * RES * RES * RES * CH
@@ -54,50 +56,79 @@ def tile_net2_pa_kernel(
         right_codes = keep.tile([P, CH, RES], U32, align_bytes=64)
         right_scales = keep.tile([P, CH, RES], U8, align_bytes=64)
         mask_kt = keep.tile([P, TILES, P, PACK], BF16)
+        means = keep.tile([P, TILES, RES], F32)
+
+        def product_pass(acc, a, c, start, stop):
+            rows = slice(a * P, (a + 1) * P)
+            nc.tensor.matmul_mx(
+                out=acc,
+                lhsT=left_codes[:, c, rows].bitcast(FP8X4),
+                lhsT_scale=left_scales[:, c, rows],
+                rhs=right_codes[:, c, :].bitcast(FP8X4),
+                rhs_scale=right_scales[:, c, :],
+                start=start,
+                stop=stop,
+            )
+
+        def mean_rows(a):
+            total = psum.tile([P, RES], F32, tag="stat")
+            for c in range(CH):
+                product_pass(total, a, c, c == 0, c == CH - 1)
+            nc.scalar.activation(out=means[:, a, :], in_=total, func=ACT.Copy, scale=1.0 / CH)
 
         with tc.tile_pool(name="loads", bufs=3) as loads, tc.tile_pool(name="work", bufs=3) as work:
-            mask_rows = loads.tile([P, TILES, RES], BF16, bufs=1)
-            nc.sync.dma_start(out=mask_rows, in_=mask.rearrange("(n r) k -> r n k", r=P))
-            for n in range(TILES):
-                mask_t = psum.tile([P, PACK, P], BF16, tag="proj", bufs=2)
-                for t in range(PACK):
-                    nc.tensor.transpose(
-                        mask_t[:, t, :], mask_rows[:, n, t * P : (t + 1) * P], ident_bf16
-                    )
-                nc.scalar.copy(out=mask_kt[:, n], in_=mask_t.rearrange("p t r -> p r t"))
-
-            def transposed_pair(rows, w, tag, bufs):
-                words = rows.bitcast(F32).rearrange("r (k w) -> r k w", w=PAIRS)
-                bank = psum.tile([P, PACK, P], F32, tag=tag, bufs=bufs)
-                for t in range(PACK):
-                    nc.tensor.transpose(bank[:, t, :], words[:, t * P : (t + 1) * P, w], ident_f32)
-                return bank.bitcast(BF16).rearrange("p t (r e) -> p e r t", e=2)
-
             sides = (
                 (right_proj, right_gate, right_codes, right_scales),
                 (left_proj, left_gate, left_codes, left_scales),
             )
             groups = [(s, n, w) for s in range(2) for n in range(TILES) for w in range(PAIRS)]
+            mask_rows = loads.tile([P, TILES, RES], BF16, bufs=1)
             loaded = {}
+            sigmoids = {}
+            transposed = {}
             gated = {}
             masked = {}
 
-            def gate_group(g):
+            def load_rows(g):
+                s, n, w = groups[g]
+                for which in (1, 0):
+                    rows = loads.tile([P, RES * CH], BF16, tag="rows%d" % which)
+                    nc.sync.dma_start(
+                        out=rows, in_=sides[s][which][n * P : (n + 1) * P].rearrange("r k c -> r (k c)")
+                    )
+                    loaded[(which, s, n)] = rows
+
+            def transposed_pair(which, g):
+                s, n, w = groups[g]
+                words = loaded[(which, s, n)].bitcast(F32).rearrange("r (k w) -> r k w", w=PAIRS)
+                bank = psum.tile([P, PACK, P], F32, tag="bank", bufs=BANKS)
+                for t in range(PACK):
+                    nc.tensor.transpose(bank[:, t, :], words[:, t * P : (t + 1) * P, w], ident_f32)
+                return bank.bitcast(BF16).rearrange("p t (r e) -> p e r t", e=2)
+
+            def sigmoid_group(g):
+                sig = work.tile([P, 2, P, PACK], F32, tag="sig", bufs=LEAD + 2)
+                nc.scalar.activation(out=sig, in_=transposed_pair(1, g), func=ACT.Sigmoid)
+                sigmoids[g] = sig
+
+            def transpose_mask(n):
+                mask_t = psum.tile([P, PACK, P], BF16, tag="stat")
+                for t in range(PACK):
+                    nc.tensor.transpose(mask_t[:, t, :], mask_rows[:, n, t * P : (t + 1) * P], ident_bf16)
+                nc.scalar.copy(out=mask_kt[:, n], in_=mask_t.rearrange("p t r -> p r t"))
+
+            def prepare_group(g):
                 s, n, w = groups[g]
                 if w == 0:
-                    gate_rows = loads.tile([P, RES * CH], BF16, tag="gate_rows")
-                    proj_rows = loads.tile([P, RES * CH], BF16, tag="proj_rows")
-                    rows = slice(n * P, (n + 1) * P)
-                    nc.sync.dma_start(out=gate_rows, in_=sides[s][1][rows].rearrange("r k c -> r (k c)"))
-                    nc.sync.dma_start(out=proj_rows, in_=sides[s][0][rows].rearrange("r k c -> r (k c)"))
-                    loaded[(s, n)] = (proj_rows, gate_rows)
-                proj_rows, gate_rows = loaded[(s, n)]
-                gate_t = transposed_pair(gate_rows, w, "aux", 3)
-                proj_t = transposed_pair(proj_rows, w, "proj", 2)
-                sig = work.tile([P, 2, P, PACK], F32, tag="sig")
-                nc.scalar.activation(out=sig, in_=gate_t, func=ACT.Sigmoid)
+                    load_rows(g)
+                sigmoid_group(g)
+                transposed[g] = transposed_pair(0, g)
+                if s == 0 and w == 0:
+                    transpose_mask(n)
+
+            def gate_group(g):
                 product = work.tile([P, 2, P, PACK], BF16, tag="product")
-                nc.vector.tensor_tensor(out=product, in0=proj_t, in1=sig, op=ALU.mult)
+                nc.vector.tensor_tensor(out=product, in0=transposed[g], in1=sigmoids[g], op=ALU.mult)
                 gated[g] = product
 
             def mask_group(g):
@@ -120,8 +151,20 @@ def tile_net2_pa_kernel(
                         scales=sides[s][3][:, 2 * w + e, rows],
                         in_=masked[g][:, e].rearrange("p r t -> p (r t)"),
                     )
+                if s == 1 and w == PAIRS - 1:
+                    mean_rows(n)
+
+            load_rows(0)
+            nc.sync.dma_start(out=mask_rows, in_=mask.rearrange("(n r) k -> r n k", r=P))
+            for g in range(LEAD):
+                sigmoid_group(g)
+            for g in range(LEAD):
+                transposed[g] = transposed_pair(0, g)
+            transpose_mask(0)
 
             for g in range(len(groups) + 2):
+                if g + LEAD < len(groups):
+                    prepare_group(g + LEAD)
                 if g < len(groups):
                     gate_group(g)
                 if 1 <= g <= len(groups):
@@ -130,38 +173,18 @@ def tile_net2_pa_kernel(
                     quantise_group(g - 2)
 
         with tc.tile_pool(name="norm", bufs=2) as norm:
-            means = {}
             planes = {}
             squares = {}
+            rstds_t = {}
             rstds = {}
 
-            def product_pass(acc, a, c, start, stop):
-                rows = slice(a * P, (a + 1) * P)
-                nc.tensor.matmul_mx(
-                    out=acc,
-                    lhsT=left_codes[:, c, rows].bitcast(FP8X4),
-                    lhsT_scale=left_scales[:, c, rows],
-                    rhs=right_codes[:, c, :].bitcast(FP8X4),
-                    rhs_scale=right_scales[:, c, :],
-                    start=start,
-                    stop=stop,
-                )
-
-            def mean_rows(a):
-                total = psum.tile([P, RES], F32, tag="sum", bufs=1)
-                for c in range(CH):
-                    product_pass(total, a, c, c == 0, c == CH - 1)
-                mean = norm.tile([P, RES], F32, tag="mean")
-                nc.scalar.activation(out=mean, in_=total, func=ACT.Copy, scale=1.0 / CH)
-                means[a] = mean
-
             def centre_rows(a):
-                centred = norm.tile([P, CH, RES], F32, tag="centred", bufs=3)
+                centred = norm.tile([P, CH, RES], F32, tag="centred", bufs=4)
                 squared = norm.tile([P, CH, RES], F32, tag="squared")
                 for c in range(CH):
-                    x = psum.tile([P, RES], F32, tag="x", bufs=2)
+                    x = psum.tile([P, RES], F32, tag="bank", bufs=BANKS)
                     product_pass(x, a, c, True, True)
-                    nc.vector.tensor_tensor(out=centred[:, c, :], in0=x, in1=means[a], op=ALU.subtract)
+                    nc.vector.tensor_tensor(out=centred[:, c, :], in0=x, in1=means[:, a, :], op=ALU.subtract)
                     if c % 2 == 1:
                         nc.scalar.activation(
                             out=squared[:, c - 1 : c + 1, :], in_=centred[:, c - 1 : c + 1, :], func=ACT.Square
@@ -169,8 +192,8 @@ def tile_net2_pa_kernel(
                 planes[a] = centred
                 squares[a] = squared
 
-            def rstd_rows(a):
-                var_t = psum.tile([P, TILES, P], F32, tag="aux", bufs=3)
+            def variance_rows(a):
+                var_t = psum.tile([P, TILES, P], F32, tag="stat")
                 for b in range(TILES):
                     for c in range(CH):
                         nc.tensor.matmul(
@@ -185,31 +208,34 @@ def tile_net2_pa_kernel(
                 nc.scalar.activation(
                     out=rstd_t, in_=var_t, func=ACT.Abs_reciprocal_sqrt, scale=1.0 / CH, bias=eps
                 )
-                rstd = psum.tile([P, TILES, P], F32, tag="aux", bufs=3)
+                rstds_t[a] = rstd_t
+
+            def rstd_rows(a):
+                rstd = psum.tile([P, TILES, P], F32, tag="rstd")
                 for b in range(TILES):
-                    nc.tensor.transpose(rstd[:, b, :], rstd_t[:, b, :], ident_f32)
+                    nc.tensor.transpose(rstd[:, b, :], rstds_t[a][:, b, :], ident_f32)
                 rstds[a] = rstd.rearrange("p b j -> p (b j)")
 
             def normalise_rows(a):
                 centred = planes[a]
-                halves = [slice(h * HALF, (h + 1) * HALF) for h in range(RES // HALF)]
-                for cols in halves:
+                for q in range(0, CH, QUAD):
                     nc.vector.tensor_tensor(
-                        out=centred[:, :, cols],
-                        in0=centred[:, :, cols],
-                        in1=rstds[a][:, cols].unsqueeze(1).to_broadcast([P, CH, HALF]),
+                        out=centred[:, q : q + QUAD, :],
+                        in0=centred[:, q : q + QUAD, :],
+                        in1=rstds[a].unsqueeze(1).to_broadcast([P, QUAD, RES]),
                         op=ALU.mult,
                     )
-                for cols in halves:
-                    for c in range(CH):
-                        nc.vector.tensor_scalar(
-                            out=centred[:, c, cols],
-                            in0=centred[:, c, cols],
-                            scalar1=gain[:, c : c + 1],
-                            scalar2=bias[:, c : c + 1],
-                            op0=ALU.mult,
-                            op1=ALU.add,
-                        )
+                for c in range(CH):
+                    nc.vector.tensor_scalar(
+                        out=centred[:, c, :],
+                        in0=centred[:, c, :],
+                        scalar1=gain[:, c : c + 1],
+                        scalar2=bias[:, c : c + 1],
+                        op0=ALU.mult,
+                        op1=ALU.add,
+                    )
+                for h in range(RES // HALF):
+                    cols = slice(h * HALF, (h + 1) * HALF)
                     result = norm.tile([P, HALF, CH], F32, tag="result", bufs=3)
                     for q in range(0, CH, QUAD):
                         nc.scalar.copy(
@@ -221,15 +247,13 @@ def tile_net2_pa_kernel(
                         in_=result.rearrange("p j c -> p (j c)"),
                     )
 
-            mean_rows(0)
             centre_rows(0)
-            mean_rows(1)
-            rstd_rows(0)
+            centre_rows(1)
+            variance_rows(0)
             for a in range(TILES):
-                if a + 1 < TILES:
-                    centre_rows(a + 1)
                 if a + 2 < TILES:
-                    mean_rows(a + 2)
+                    centre_rows(a + 2)
+                rstd_rows(a)
                 if a + 1 < TILES:
-                    rstd_rows(a + 1)
+                    variance_rows(a + 1)
                 normalise_rows(a)

@@ -20,6 +20,7 @@ TILES = RES // P
 HALF = RES // 2
 QUAD = 4
 LEAD = 2
+SIG_LEAD = 3
 BANKS = 6
 EPS = 1e-5
 
@@ -76,7 +77,8 @@ def tile_net2_pa_kernel(
                 product_pass(total, a, c, c == 0, c == CH - 1)
             nc.scalar.activation(out=means[:, a, :], in_=total, func=ACT.Copy, scale=1.0 / CH)
 
-        with tc.tile_pool(name="loads", bufs=3) as loads, tc.tile_pool(name="work", bufs=3) as work:
+        work = ctx.enter_context(tc.tile_pool(name="work", bufs=3))
+        with tc.tile_pool(name="loads", bufs=3) as loads:
             sides = (
                 (right_proj, right_gate, right_codes, right_scales),
                 (left_proj, left_gate, left_codes, left_scales),
@@ -107,7 +109,7 @@ def tile_net2_pa_kernel(
                 return bank.bitcast(BF16).rearrange("p t (r e) -> p e r t", e=2)
 
             def sigmoid_group(g):
-                sig = work.tile([P, 2, P, PACK], F32, tag="sig", bufs=LEAD + 2)
+                sig = work.tile([P, 2, P, PACK], F32, tag="sig", bufs=SIG_LEAD + 2)
                 nc.scalar.activation(out=sig, in_=transposed_pair(1, g), func=ACT.Sigmoid)
                 sigmoids[g] = sig
 
@@ -117,24 +119,32 @@ def tile_net2_pa_kernel(
                     nc.tensor.transpose(mask_t[:, t, :], mask_rows[:, n, t * P : (t + 1) * P], ident_bf16)
                 nc.scalar.copy(out=mask_kt[:, n], in_=mask_t.rearrange("p t r -> p r t"))
 
-            def prepare_group(g):
+            def prepare_sigmoid(g):
                 s, n, w = groups[g]
                 if w == 0:
                     load_rows(g)
                 sigmoid_group(g)
+
+            def prepare_projection(g):
+                s, n, w = groups[g]
                 transposed[g] = transposed_pair(0, g)
                 if s == 0 and w == 0:
                     transpose_mask(n)
 
             def gate_group(g):
-                product = work.tile([P, 2, P, PACK], BF16, tag="product")
+                product = work.tile([P, 2, P, PACK], BF16, tag="product", bufs=2 * PAIRS)
                 nc.vector.tensor_tensor(out=product, in0=transposed[g], in1=sigmoids[g], op=ALU.mult)
                 gated[g] = product
 
             def mask_group(g):
                 s, n, w = groups[g]
-                kept = work.tile([P, 2, P, PACK], BF16, tag="kept", align_bytes=64)
-                nc.vector.tensor_tensor(
+                if w < PAIRS // 2:
+                    engine = nc.vector
+                    kept = work.tile([P, 2, P, PACK], BF16, tag="kept_vector", bufs=PAIRS, align_bytes=64)
+                else:
+                    engine = nc.gpsimd
+                    kept = work.tile([P, 2, P, PACK], BF16, tag="kept_gpsimd", bufs=PAIRS // 2, align_bytes=64)
+                engine.tensor_tensor(
                     out=kept,
                     in0=gated[g],
                     in1=mask_kt[:, n].unsqueeze(1).to_broadcast([P, 2, P, PACK]),
@@ -151,7 +161,14 @@ def tile_net2_pa_kernel(
                         scales=sides[s][3][:, 2 * w + e, rows],
                         in_=masked[g][:, e].rearrange("p r t -> p (r t)"),
                     )
-                if s == 1 and w == PAIRS - 1:
+
+            def quantise_tile(first):
+                for g in range(first, first + PAIRS):
+                    quantise_group(g)
+
+            def mean_of_tile(first):
+                s, n, w = groups[first]
+                if s == 1:
                     mean_rows(n)
 
             load_rows(0)
@@ -161,16 +178,22 @@ def tile_net2_pa_kernel(
             for g in range(LEAD):
                 transposed[g] = transposed_pair(0, g)
             transpose_mask(0)
+            for g in range(LEAD, SIG_LEAD):
+                sigmoid_group(g)
 
-            for g in range(len(groups) + 2):
-                if g + LEAD < len(groups):
-                    prepare_group(g + LEAD)
-                if g < len(groups):
+            for first in range(0, len(groups), PAIRS):
+                for g in range(first, first + PAIRS):
+                    if g + LEAD < len(groups):
+                        prepare_projection(g + LEAD)
+                    if g + SIG_LEAD < len(groups):
+                        prepare_sigmoid(g + SIG_LEAD)
                     gate_group(g)
-                if 1 <= g <= len(groups):
-                    mask_group(g - 1)
-                if g >= 2:
-                    quantise_group(g - 2)
+                for g in range(first, first + PAIRS):
+                    mask_group(g)
+                if first >= PAIRS:
+                    quantise_tile(first - PAIRS)
+                if first >= 2 * PAIRS:
+                    mean_of_tile(first - 2 * PAIRS)
 
         with tc.tile_pool(name="norm", bufs=2) as norm:
             planes = {}
@@ -248,11 +271,15 @@ def tile_net2_pa_kernel(
                     )
 
             centre_rows(0)
+            quantise_tile(len(groups) - PAIRS)
+            mean_of_tile(len(groups) - 2 * PAIRS)
             centre_rows(1)
             variance_rows(0)
             for a in range(TILES):
                 if a + 2 < TILES:
                     centre_rows(a + 2)
+                if a + 3 < TILES:
+                    mean_rows(a + 3)
                 rstd_rows(a)
                 if a + 1 < TILES:
                     variance_rows(a + 1)

@@ -22,6 +22,7 @@ QUAD = 4
 LEAD = 2
 SIG_LEAD = 3
 BANKS = 6
+S_SHARE = 224
 EPS = 1e-5
 
 FLOPS = 2 * RES * RES * RES * CH
@@ -195,6 +196,9 @@ def tile_net2_pa_kernel(
                 if first >= 2 * PAIRS:
                     mean_of_tile(first - 2 * PAIRS)
 
+        warm = keep.tile([P, 1], F32)
+        nc.scalar.activation(out=warm, in_=eps, func=ACT.Abs_reciprocal_sqrt)
+
         with tc.tile_pool(name="norm", bufs=2) as norm:
             planes = {}
             squares = {}
@@ -239,36 +243,47 @@ def tile_net2_pa_kernel(
                     nc.tensor.transpose(rstd[:, b, :], rstds_t[a][:, b, :], ident_f32)
                 rstds[a] = rstd.rearrange("p b j -> p (b j)")
 
-            def normalise_rows(a):
+            def normalise_half(a, h):
                 centred = planes[a]
-                for q in range(0, CH, QUAD):
-                    nc.vector.tensor_tensor(
-                        out=centred[:, q : q + QUAD, :],
-                        in0=centred[:, q : q + QUAD, :],
-                        in1=rstds[a].unsqueeze(1).to_broadcast([P, QUAD, RES]),
-                        op=ALU.mult,
-                    )
+                cols = slice(h * HALF, (h + 1) * HALF)
+                nc.vector.tensor_tensor(
+                    out=centred[:, :, cols],
+                    in0=centred[:, :, cols],
+                    in1=rstds[a][:, cols].unsqueeze(1).to_broadcast([P, CH, HALF]),
+                    op=ALU.mult,
+                )
                 for c in range(CH):
-                    nc.vector.tensor_scalar(
-                        out=centred[:, c, :],
-                        in0=centred[:, c, :],
+                    affine_engine = nc.gpsimd if c < QUAD else nc.vector
+                    affine_engine.tensor_scalar(
+                        out=centred[:, c, cols],
+                        in0=centred[:, c, cols],
                         scalar1=gain[:, c : c + 1],
                         scalar2=bias[:, c : c + 1],
                         op0=ALU.mult,
                         op1=ALU.add,
                     )
-                for h in range(RES // HALF):
-                    cols = slice(h * HALF, (h + 1) * HALF)
-                    result = norm.tile([P, HALF, CH], F32, tag="result", bufs=3)
-                    for q in range(0, CH, QUAD):
-                        nc.scalar.copy(
-                            out=result[:, :, q : q + QUAD],
-                            in_=centred[:, q : q + QUAD, cols].rearrange("p c j -> p j c"),
-                        )
-                    nc.sync.dma_start(
-                        out=out[a * P : (a + 1) * P, cols, :].rearrange("i j c -> i (j c)"),
-                        in_=result.rearrange("p j c -> p (j c)"),
+
+            def store_half(a, h):
+                centred = planes[a]
+                first = h * HALF
+                result = norm.tile([P, HALF, CH], F32, tag="result", bufs=3)
+                for q in range(0, CH, QUAD):
+                    nc.scalar.copy(
+                        out=result[:, 0:S_SHARE, q : q + QUAD],
+                        in_=centred[:, q : q + QUAD, first : first + S_SHARE].rearrange("p c j -> p j c"),
                     )
+                    nc.gpsimd.tensor_scalar(
+                        out=result[:, S_SHARE:HALF, q : q + QUAD],
+                        in0=centred[:, q : q + QUAD, first + S_SHARE : first + HALF].rearrange("p c j -> p j c"),
+                        scalar1=1.0,
+                        scalar2=0.0,
+                        op0=ALU.mult,
+                        op1=ALU.add,
+                    )
+                nc.sync.dma_start(
+                    out=out[a * P : (a + 1) * P, first : first + HALF, :].rearrange("i j c -> i (j c)"),
+                    in_=result.rearrange("p j c -> p (j c)"),
+                )
 
             centre_rows(0)
             quantise_tile(len(groups) - PAIRS)
@@ -283,4 +298,9 @@ def tile_net2_pa_kernel(
                 rstd_rows(a)
                 if a + 1 < TILES:
                     variance_rows(a + 1)
-                normalise_rows(a)
+                normalise_half(a, 0)
+                if a >= 1:
+                    store_half(a - 1, 1)
+                normalise_half(a, 1)
+                store_half(a, 0)
+            store_half(TILES - 1, 1)

from contextlib import ExitStack

import concourse.mybir as mybir
from concourse.masks import make_identity

BF16 = mybir.dt.bfloat16
F32 = mybir.dt.float32
U32 = mybir.dt.uint32
U8 = mybir.dt.uint8
FP8X4 = mybir.dt.float8_e4m3fn_x4
ACT = mybir.ActivationFunctionType
ALU = mybir.AluOpType

P = 128
PACK = 4
RES = 512
CH = 8
PAIRS = CH // 2
TILES = RES // P
HALF = RES // 2
QUAD = 4
LEAD = 2
SIG_LEAD = 3
BANKS = 6
S_SHARE = 224
EPS = 1e-5

FLOPS = 2 * RES * RES * RES * CH


def tile_net2_pa_kernel(
    tc, left_proj, left_gate, right_proj, right_gate, mask, ln_c_g, ln_c_b, out
):
    nc = tc.nc
    with ExitStack() as ctx:
        ctx.enter_context(tc.manual_schedule())
        keep = ctx.enter_context(tc.tile_pool(name="keep", bufs=1))
        psum = ctx.enter_context(tc.psum_pool(name="psum", bufs=1))

        ident_f32 = keep.tile([P, P], F32)
        make_identity(nc, ident_f32)
        ident_bf16 = keep.tile([P, P], BF16)
        make_identity(nc, ident_bf16)

        gain_bf16 = keep.tile([P, CH], BF16)
        nc.scalar.dma_start(out=gain_bf16, in_=ln_c_g.partition_broadcast(P))
        bias_bf16 = keep.tile([P, CH], BF16)
        nc.scalar.dma_start(out=bias_bf16, in_=ln_c_b.partition_broadcast(P))
        gain = keep.tile([P, CH], F32)
        nc.vector.tensor_copy(out=gain, in_=gain_bf16)
        bias = keep.tile([P, CH], F32)
        nc.vector.tensor_copy(out=bias, in_=bias_bf16)
        eps = keep.tile([P, 1], F32)
        nc.vector.memset(eps, EPS)

        left_codes = keep.tile([P, CH, RES], U32, align_bytes=64)
        left_scales = keep.tile([P, CH, RES], U8, align_bytes=64)
        right_codes = keep.tile([P, CH, RES], U32, align_bytes=64)
        right_scales = keep.tile([P, CH, RES], U8, align_bytes=64)
        mask_kt = keep.tile([P, TILES, P, PACK], BF16)
        means = keep.tile([P, TILES, RES], F32)

        def product_pass(acc, a, c, start, stop):
            rows = slice(a * P, (a + 1) * P)
            nc.tensor.matmul_mx(
                out=acc,
                lhsT=left_codes[:, c, rows].bitcast(FP8X4),
                lhsT_scale=left_scales[:, c, rows],
                rhs=right_codes[:, c, :].bitcast(FP8X4),
                rhs_scale=right_scales[:, c, :],
                start=start,
                stop=stop,
            )

        def mean_rows(a):
            total = psum.tile([P, RES], F32, tag="stat")
            for c in range(CH):
                product_pass(total, a, c, c == 0, c == CH - 1)
            nc.scalar.activation(out=means[:, a, :], in_=total, func=ACT.Copy, scale=1.0 / CH)

        work = ctx.enter_context(tc.tile_pool(name="work", bufs=3))
        with tc.tile_pool(name="loads", bufs=3) as loads:
            sides = (
                (right_proj, right_gate, right_codes, right_scales),
                (left_proj, left_gate, left_codes, left_scales),
            )
            groups = [(s, n, w) for s in range(2) for n in range(TILES) for w in range(PAIRS)]
            mask_rows = loads.tile([P, TILES, RES], BF16, bufs=1)
            loaded = {}
            sigmoids = {}
            transposed = {}
            gated = {}
            masked = {}

            def load_rows(g):
                s, n, w = groups[g]
                for which in (1, 0):
                    rows = loads.tile([P, RES * CH], BF16, tag="rows%d" % which)
                    nc.sync.dma_start(
                        out=rows, in_=sides[s][which][n * P : (n + 1) * P].rearrange("r k c -> r (k c)")
                    )
                    loaded[(which, s, n)] = rows

            def transposed_pair(which, g):
                s, n, w = groups[g]
                words = loaded[(which, s, n)].bitcast(F32).rearrange("r (k w) -> r k w", w=PAIRS)
                bank = psum.tile([P, PACK, P], F32, tag="bank", bufs=BANKS)
                for t in range(PACK):
                    nc.tensor.transpose(bank[:, t, :], words[:, t * P : (t + 1) * P, w], ident_f32)
                return bank.bitcast(BF16).rearrange("p t (r e) -> p e r t", e=2)

            def sigmoid_group(g):
                sig = work.tile([P, 2, P, PACK], F32, tag="sig", bufs=SIG_LEAD + 2)
                nc.scalar.activation(out=sig, in_=transposed_pair(1, g), func=ACT.Sigmoid)
                sigmoids[g] = sig

            def transpose_mask(n):
                mask_t = psum.tile([P, PACK, P], BF16, tag="stat")
                for t in range(PACK):
                    nc.tensor.transpose(mask_t[:, t, :], mask_rows[:, n, t * P : (t + 1) * P], ident_bf16)
                nc.scalar.copy(out=mask_kt[:, n], in_=mask_t.rearrange("p t r -> p r t"))

            def prepare_sigmoid(g):
                s, n, w = groups[g]
                if w == 0:
                    load_rows(g)
                sigmoid_group(g)

            def prepare_projection(g):
                s, n, w = groups[g]
                transposed[g] = transposed_pair(0, g)
                if s == 0 and w == 0:
                    transpose_mask(n)

            def gate_group(g):
                product = work.tile([P, 2, P, PACK], BF16, tag="product", bufs=2 * PAIRS)
                nc.vector.tensor_tensor(out=product, in0=transposed[g], in1=sigmoids[g], op=ALU.mult)
                gated[g] = product

            def mask_group(g):
                s, n, w = groups[g]
                if w < PAIRS // 2:
                    engine = nc.vector
                    kept = work.tile([P, 2, P, PACK], BF16, tag="kept_vector", bufs=PAIRS, align_bytes=64)
                else:
                    engine = nc.gpsimd
                    kept = work.tile([P, 2, P, PACK], BF16, tag="kept_gpsimd", bufs=PAIRS // 2, align_bytes=64)
                engine.tensor_tensor(
                    out=kept,
                    in0=gated[g],
                    in1=mask_kt[:, n].unsqueeze(1).to_broadcast([P, 2, P, PACK]),
                    op=ALU.mult,
                )
                masked[g] = kept

            def quantise_group(g):
                s, n, w = groups[g]
                rows = slice(n * P, (n + 1) * P)
                for e in range(2):
                    nc.vector.quantize_mx(
                        out=sides[s][2][:, 2 * w + e, rows].bitcast(FP8X4),
                        scales=sides[s][3][:, 2 * w + e, rows],
                        in_=masked[g][:, e].rearrange("p r t -> p (r t)"),
                    )

            def quantise_tile(first):
                for g in range(first, first + PAIRS):
                    quantise_group(g)

            def mean_of_tile(first):
                s, n, w = groups[first]
                if s == 1:
                    mean_rows(n)

            load_rows(0)
            nc.sync.dma_start(out=mask_rows, in_=mask.rearrange("(n r) k -> r n k", r=P))
            for g in range(LEAD):
                sigmoid_group(g)
            for g in range(LEAD):
                transposed[g] = transposed_pair(0, g)
            transpose_mask(0)
            for g in range(LEAD, SIG_LEAD):
                sigmoid_group(g)

            for first in range(0, len(groups), PAIRS):
                for g in range(first, first + PAIRS):
                    if g + LEAD < len(groups):
                        prepare_projection(g + LEAD)
                    if g + SIG_LEAD < len(groups):
                        prepare_sigmoid(g + SIG_LEAD)
                    gate_group(g)
                for g in range(first, first + PAIRS):
                    mask_group(g)
                if first >= PAIRS:
                    quantise_tile(first - PAIRS)
                if first >= 2 * PAIRS:
                    mean_of_tile(first - 2 * PAIRS)

        warm = keep.tile([P, 1], F32)
        nc.scalar.activation(out=warm, in_=eps, func=ACT.Abs_reciprocal_sqrt)

        with tc.tile_pool(name="norm", bufs=2) as norm:
            planes = {}
            squares = {}
            rstds_t = {}
            rstds = {}

            def centre_rows(a):
                centred = norm.tile([P, CH, RES], F32, tag="centred", bufs=4)
                squared = norm.tile([P, CH, RES], F32, tag="squared")
                for c in range(CH):
                    x = psum.tile([P, RES], F32, tag="bank", bufs=BANKS)
                    product_pass(x, a, c, True, True)
                    nc.vector.tensor_tensor(out=centred[:, c, :], in0=x, in1=means[:, a, :], op=ALU.subtract)
                    if c % 2 == 1:
                        nc.scalar.activation(
                            out=squared[:, c - 1 : c + 1, :], in_=centred[:, c - 1 : c + 1, :], func=ACT.Square
                        )
                planes[a] = centred
                squares[a] = squared

            def variance_rows(a):
                var_t = psum.tile([P, TILES, P], F32, tag="stat")
                for b in range(TILES):
                    for c in range(CH):
                        nc.tensor.matmul(
                            out=var_t[:, b, :],
                            lhsT=squares[a][:, c, b * P : (b + 1) * P],
                            rhs=ident_f32,
                            is_transpose=True,
                            start=(c == 0),
                            stop=(c == CH - 1),
                        )
                rstd_t = norm.tile([P, TILES, P], F32, tag="rstd_t")
                nc.scalar.activation(
                    out=rstd_t, in_=var_t, func=ACT.Abs_reciprocal_sqrt, scale=1.0 / CH, bias=eps
                )
                rstds_t[a] = rstd_t

            def rstd_rows(a):
                rstd = psum.tile([P, TILES, P], F32, tag="rstd")
                for b in range(TILES):
                    nc.tensor.transpose(rstd[:, b, :], rstds_t[a][:, b, :], ident_f32)
                rstds[a] = rstd.rearrange("p b j -> p (b j)")

            def normalise_half(a, h):
                centred = planes[a]
                cols = slice(h * HALF, (h + 1) * HALF)
                nc.vector.tensor_tensor(
                    out=centred[:, :, cols],
                    in0=centred[:, :, cols],
                    in1=rstds[a][:, cols].unsqueeze(1).to_broadcast([P, CH, HALF]),
                    op=ALU.mult,
                )
                for c in range(CH):
                    affine_engine = nc.gpsimd if c < QUAD else nc.vector
                    affine_engine.tensor_scalar(
                        out=centred[:, c, cols],
                        in0=centred[:, c, cols],
                        scalar1=gain[:, c : c + 1],
                        scalar2=bias[:, c : c + 1],
                        op0=ALU.mult,
                        op1=ALU.add,
                    )

            def store_half(a, h):
                centred = planes[a]
                first = h * HALF
                result = norm.tile([P, HALF, CH], F32, tag="result", bufs=3)
                for q in range(0, CH, QUAD):
                    nc.scalar.copy(
                        out=result[:, 0:S_SHARE, q : q + QUAD],
                        in_=centred[:, q : q + QUAD, first : first + S_SHARE].rearrange("p c j -> p j c"),
                    )
                    nc.gpsimd.tensor_scalar(
                        out=result[:, S_SHARE:HALF, q : q + QUAD],
                        in0=centred[:, q : q + QUAD, first + S_SHARE : first + HALF].rearrange("p c j -> p j c"),
                        scalar1=1.0,
                        scalar2=0.0,
                        op0=ALU.mult,
                        op1=ALU.add,
                    )
                nc.sync.dma_start(
                    out=out[a * P : (a + 1) * P, first : first + HALF, :].rearrange("i j c -> i (j c)"),
                    in_=result.rearrange("p j c -> p (j c)"),
                )

            centre_rows(0)
            quantise_tile(len(groups) - PAIRS)
            mean_of_tile(len(groups) - 2 * PAIRS)
            centre_rows(1)
            variance_rows(0)
            for a in range(TILES):
                if a + 2 < TILES:
                    centre_rows(a + 2)
                if a + 3 < TILES:
                    mean_rows(a + 3)
                rstd_rows(a)
                if a + 1 < TILES:
                    variance_rows(a + 1)
                normalise_half(a, 0)
                if a >= 1:
                    store_half(a - 1, 1)
                normalise_half(a, 1)
                store_half(a, 0)
            store_half(TILES - 1, 1)
